import numpy as np
import ml_dtypes

BF16 = ml_dtypes.bfloat16


def bf(x):
    return np.asarray(x, np.float32).astype(BF16)


def f32(x):
    return np.asarray(x, np.float32)


def f64(x):
    return np.asarray(x).astype(np.float64)


def striped(idx):
    return np.tile(idx.reshape(-1, 16).T, (8, 1))


C, S, B, T, N = 128, 1024, 4, 256, 1024
EPS = 1e-5
BASE = 10000.0


def pos_enc():
    pos = np.arange(T, dtype=np.float32)[None, :]
    two_i = np.arange(0, C, 2, dtype=np.float32)[:, None]
    angle = f64(pos / np.power(np.float32(BASE), two_i / np.float32(C)))
    pe = np.zeros((C, T))
    pe[0::2] = np.sin(angle)
    pe[1::2] = np.cos(angle)
    return f32(pe)


def setup_inputs():
    return {"table": f32(np.random.standard_normal((C, S))), "pe": pos_enc(), "bp": f32(0.1 * np.random.standard_normal((C, 1))), "gamma": f32(1.0 + 0.1 * np.random.standard_normal((C, 1))), "beta": f32(0.1 * np.random.standard_normal((C, 1))), "offs": striped(np.random.permutation(np.tile(np.arange(S), 2))[:N])}


def reference(table, pe, bp, gamma, beta, offs):
    idx = offs[:16].T.reshape(-1)
    e = f64(table)[:, idx] / np.sqrt(B) + np.tile(f64(pe), (1, B)) + f64(bp)
    mu = e.mean(axis=0, keepdims=True)
    var = np.square(e - mu).mean(axis=0, keepdims=True)
    return f64(gamma) * (e - mu) / np.sqrt(var + EPS) + f64(beta)

@@ -1,0 +1,80 @@
+import concourse.mybir as mybir
+
+F32 = mybir.dt.float32
+U16 = mybir.dt.uint16
+ALU = mybir.AluOpType
+FUNC = mybir.ActivationFunctionType
+
+FEATURES = 128
+WORDS = 1024
+TOKENS = 256
+SENTENCES = 4
+EPS = 1e-5
+OFFSETS_PER_COLUMN = 16
+
+FLOPS = 2 * 2 * FEATURES * FEATURES * SENTENCES * TOKENS
+
+
+def tile_transformertranslator_kernel(tc, table, pe, bp, gamma, beta, offs, out):
+    nc = tc.nc
+    with (
+        tc.tile_pool(name="held", bufs=1) as held,
+        tc.tile_pool(name="work", bufs=SENTENCES) as work,
+        tc.psum_pool(name="psum", bufs=SENTENCES) as psum,
+    ):
+        offsets = held.tile([FEATURES, SENTENCES * TOKENS // OFFSETS_PER_COLUMN], U16, name="offsets")
+        nc.sync.dma_start(offsets[:], offs)
+        words = held.tile([FEATURES, WORDS], F32, name="words")
+        nc.sync.dma_start(words[:], table)
+        position = held.tile([FEATURES, TOKENS], F32, name="position")
+        nc.scalar.dma_start(position[:], pe)
+        bias = held.tile([FEATURES, 1], F32, name="bias")
+        nc.scalar.dma_start(bias[:], bp)
+        gain = held.tile([FEATURES, 1], F32, name="gain")
+        nc.scalar.dma_start(gain[:], gamma)
+        shift = held.tile([FEATURES, 1], F32, name="shift")
+        nc.scalar.dma_start(shift[:], beta)
+
+        centre = held.tile([FEATURES, FEATURES], F32, name="centre")
+        nc.gpsimd.memset(centre[:], -1.0 / FEATURES)
+        nc.gpsimd.affine_select(
+            out=centre[:],
+            in_=centre[:],
+            pattern=[[-1, FEATURES]],
+            compare_op=ALU.not_equal,
+            fill=1.0 - 1.0 / FEATURES,
+            base=0,
+            channel_multiplier=1,
+        )
+        average = held.tile([FEATURES, FEATURES], F32, name="average")
+        nc.gpsimd.memset(average[:], 1.0 / FEATURES)
+        four_eps = held.tile([FEATURES, 1], F32, name="four_eps")
+        nc.gpsimd.memset(four_eps[:], 4.0 * EPS)
+
+        added = held.tile([FEATURES, TOKENS], F32, name="added")
+        nc.vector.tensor_scalar(added[:], position[:], bias[:, 0:1], 2.0, ALU.add, ALU.mult)
+
+        columns = TOKENS // OFFSETS_PER_COLUMN
+        for s in range(SENTENCES):
+            doubled = work.tile([FEATURES, TOKENS], F32, name="doubled")
+            nc.vector.tensor_tensor(
+                doubled[:],
+                words[:].indirect(offsets[:, s * columns : (s + 1) * columns]),
+                added[:],
+                ALU.add,
+            )
+            centred = psum.tile([FEATURES, TOKENS], F32, name="centred")
+            nc.tensor.matmul(centred[:], centre[:], doubled[:], start=True, stop=True)
+            squared = work.tile([FEATURES, TOKENS], F32, name="squared")
+            nc.scalar.activation(squared[:], centred[:], FUNC.Square)
+            var = psum.tile([FEATURES, TOKENS], F32, name="var")
+            nc.tensor.matmul(var[:], average[:], squared[:], start=True, stop=True)
+            rstd = work.tile([FEATURES, TOKENS], F32, name="rstd")
+            nc.scalar.activation(rstd[:], var[:], FUNC.Abs_reciprocal_sqrt, bias=four_eps[:, 0:1])
+            normed = work.tile([FEATURES, TOKENS], F32, name="normed")
+            nc.vector.tensor_tensor(normed[:], centred[:], rstd[:], ALU.mult)
+            result = work.tile([FEATURES, TOKENS], F32, name="result")
+            nc.scalar.activation(
+                result[:], normed[:], FUNC.Identity, bias=shift[:, 0:1], scale=gain[:, 0:1]
+            )
+            nc.sync.dma_start(out[:, s * TOKENS : (s + 1) * TOKENS], result[:])

@@ -11,6 +11,9 @@ TOKENS = 256
 SENTENCES = 4
 EPS = 1e-5
 OFFSETS_PER_COLUMN = 16
+PIECE = 128
+PIECES = SENTENCES * TOKENS // PIECE
+WARM_UP_PRODUCTS = 10
 
 FLOPS = 2 * 2 * FEATURES * FEATURES * SENTENCES * TOKENS
 
@@ -19,8 +22,8 @@ def tile_transformertranslator_kernel(tc, table, pe, bp, gamma, beta, offs, out)
     nc = tc.nc
     with (
         tc.tile_pool(name="held", bufs=1) as held,
-        tc.tile_pool(name="work", bufs=SENTENCES) as work,
-        tc.psum_pool(name="psum", bufs=SENTENCES) as psum,
+        tc.tile_pool(name="work", bufs=PIECES) as work,
+        tc.psum_pool(name="psum", bufs=PIECES) as psum,
     ):
         offsets = held.tile([FEATURES, SENTENCES * TOKENS // OFFSETS_PER_COLUMN], U16, name="offsets")
         nc.sync.dma_start(offsets[:], offs)
@@ -51,30 +54,46 @@ def tile_transformertranslator_kernel(tc, table, pe, bp, gamma, beta, offs, out)
         four_eps = held.tile([FEATURES, 1], F32, name="four_eps")
         nc.gpsimd.memset(four_eps[:], 4.0 * EPS)
 
+        idle_product = psum.tile([FEATURES, FEATURES], F32, name="idle_product", tag="stats")
+        for repeat in range(WARM_UP_PRODUCTS):
+            nc.tensor.matmul(idle_product[:], average[:], centre[:], start=True, stop=True)
+
+        unused = held.tile([FEATURES, 1], F32, name="unused")
+        nc.scalar.activation(unused[:], four_eps[:], FUNC.Abs_reciprocal_sqrt)
+
         added = held.tile([FEATURES, TOKENS], F32, name="added")
         nc.vector.tensor_scalar(added[:], position[:], bias[:, 0:1], 2.0, ALU.add, ALU.mult)
 
-        columns = TOKENS // OFFSETS_PER_COLUMN
-        for s in range(SENTENCES):
-            doubled = work.tile([FEATURES, TOKENS], F32, name="doubled")
+        columns = PIECE // OFFSETS_PER_COLUMN
+        all_stats = []
+        all_squared = []
+        for p in range(PIECES):
+            in_sentence = p * PIECE % TOKENS
+
+            doubled = work.tile([FEATURES, PIECE], F32, name="doubled")
             nc.vector.tensor_tensor(
                 doubled[:],
-                words[:].indirect(offsets[:, s * columns : (s + 1) * columns]),
-                added[:],
+                words[:].indirect(offsets[:, p * columns : (p + 1) * columns]),
+                added[:, in_sentence : in_sentence + PIECE],
                 ALU.add,
             )
-            centred = psum.tile([FEATURES, TOKENS], F32, name="centred")
-            nc.tensor.matmul(centred[:], centre[:], doubled[:], start=True, stop=True)
-            squared = work.tile([FEATURES, TOKENS], F32, name="squared")
-            nc.scalar.activation(squared[:], centred[:], FUNC.Square)
-            var = psum.tile([FEATURES, TOKENS], F32, name="var")
-            nc.tensor.matmul(var[:], average[:], squared[:], start=True, stop=True)
-            rstd = work.tile([FEATURES, TOKENS], F32, name="rstd")
-            nc.scalar.activation(rstd[:], var[:], FUNC.Abs_reciprocal_sqrt, bias=four_eps[:, 0:1])
-            normed = work.tile([FEATURES, TOKENS], F32, name="normed")
-            nc.vector.tensor_tensor(normed[:], centred[:], rstd[:], ALU.mult)
-            result = work.tile([FEATURES, TOKENS], F32, name="result")
+            stats = psum.tile([FEATURES, 2 * PIECE], F32, name="stats")
+            nc.tensor.matmul(stats[:, 0:PIECE], centre[:], doubled[:], start=True, stop=True)
+            squared = work.tile([FEATURES, PIECE], F32, name="squared")
+            nc.scalar.activation(squared[:], stats[:, 0:PIECE], FUNC.Square)
+            all_stats.append(stats)
+            all_squared.append(squared)
+
+        for p in range(PIECES):
+            centred = all_stats[p][:, 0:PIECE]
+            var = all_stats[p][:, PIECE : 2 * PIECE]
+            nc.tensor.matmul(var, average[:], all_squared[p][:], start=True, stop=True)
+            rstd = work.tile([FEATURES, PIECE], F32, name="rstd")
+            nc.scalar.activation(rstd[:], var, FUNC.Abs_reciprocal_sqrt, bias=four_eps[:, 0:1])
+            normed = work.tile([FEATURES, PIECE], F32, name="normed")
+            nc.vector.tensor_tensor(normed[:], centred, rstd[:], ALU.mult)
+            result = work.tile([FEATURES, PIECE], F32, name="result")
             nc.scalar.activation(
                 result[:], normed[:], FUNC.Identity, bias=shift[:, 0:1], scale=gain[:, 0:1]
             )
-            nc.sync.dma_start(out[:, s * TOKENS : (s + 1) * TOKENS], result[:])
+            nc.sync.dma_start(out[:, p * PIECE : (p + 1) * PIECE], result[:])

@@ -13,7 +13,7 @@ EPS = 1e-5
 OFFSETS_PER_COLUMN = 16
 PIECE = 128
 PIECES = SENTENCES * TOKENS // PIECE
-WARM_UP_PRODUCTS = 10
+WARM_UP_PRODUCTS = 6
 
 FLOPS = 2 * 2 * FEATURES * FEATURES * SENTENCES * TOKENS
 
@@ -25,12 +25,12 @@ def tile_transformertranslator_kernel(tc, table, pe, bp, gamma, beta, offs, out)
         tc.tile_pool(name="work", bufs=PIECES) as work,
         tc.psum_pool(name="psum", bufs=PIECES) as psum,
     ):
+        position = held.tile([FEATURES, TOKENS], F32, name="position")
+        nc.sync.dma_start(position[:], pe)
         offsets = held.tile([FEATURES, SENTENCES * TOKENS // OFFSETS_PER_COLUMN], U16, name="offsets")
         nc.sync.dma_start(offsets[:], offs)
         words = held.tile([FEATURES, WORDS], F32, name="words")
         nc.sync.dma_start(words[:], table)
-        position = held.tile([FEATURES, TOKENS], F32, name="position")
-        nc.scalar.dma_start(position[:], pe)
         bias = held.tile([FEATURES, 1], F32, name="bias")
         nc.scalar.dma_start(bias[:], bp)
         gain = held.tile([FEATURES, 1], F32, name="gain")
@@ -93,7 +93,7 @@ def tile_transformertranslator_kernel(tc, table, pe, bp, gamma, beta, offs, out)
             normed = work.tile([FEATURES, PIECE], F32, name="normed")
             nc.vector.tensor_tensor(normed[:], centred, rstd[:], ALU.mult)
             result = work.tile([FEATURES, PIECE], F32, name="result")
-            nc.scalar.activation(
-                result[:], normed[:], FUNC.Identity, bias=shift[:, 0:1], scale=gain[:, 0:1]
+            nc.vector.tensor_scalar(
+                result[:], normed[:], gain[:, 0:1], shift[:, 0:1], ALU.mult, ALU.add
             )
             nc.sync.dma_start(out[:, p * PIECE : (p + 1) * PIECE], result[:])

@@ -1,4 +1,5 @@
 import concourse.mybir as mybir
+from concourse.masks import make_identity
 
 F32 = mybir.dt.float32
 U16 = mybir.dt.uint16
@@ -15,7 +16,7 @@ PIECE = 128
 PIECES = SENTENCES * TOKENS // PIECE
 WARM_UP_PRODUCTS = 6
 
-FLOPS = 2 * 2 * FEATURES * FEATURES * SENTENCES * TOKENS
+FLOPS = 2 * FEATURES * FEATURES * SENTENCES * TOKENS
 
 
 def tile_transformertranslator_kernel(tc, table, pe, bp, gamma, beta, offs, out):
@@ -49,24 +50,24 @@ def tile_transformertranslator_kernel(tc, table, pe, bp, gamma, beta, offs, out)
             base=0,
             channel_multiplier=1,
         )
-        average = held.tile([FEATURES, FEATURES], F32, name="average")
-        nc.gpsimd.memset(average[:], 1.0 / FEATURES)
-        four_eps = held.tile([FEATURES, 1], F32, name="four_eps")
+        identity = held.tile([PIECE, PIECE], F32, name="identity")
+        make_identity(nc, identity[:])
+        four_eps = held.tile([PIECE, 1], F32, name="four_eps")
         nc.gpsimd.memset(four_eps[:], 4.0 * EPS)
 
-        idle_product = psum.tile([FEATURES, FEATURES], F32, name="idle_product", tag="stats")
+        idle_product = psum.tile([FEATURES, FEATURES], F32, name="idle_product", tag="turned")
         for repeat in range(WARM_UP_PRODUCTS):
-            nc.tensor.matmul(idle_product[:], average[:], centre[:], start=True, stop=True)
+            nc.tensor.matmul(idle_product[:], centre[:], centre[:], start=True, stop=True)
 
-        unused = held.tile([FEATURES, 1], F32, name="unused")
+        unused = held.tile([PIECE, 1], F32, name="unused")
         nc.scalar.activation(unused[:], four_eps[:], FUNC.Abs_reciprocal_sqrt)
 
         added = held.tile([FEATURES, TOKENS], F32, name="added")
         nc.vector.tensor_scalar(added[:], position[:], bias[:, 0:1], 2.0, ALU.add, ALU.mult)
 
         columns = PIECE // OFFSETS_PER_COLUMN
-        all_stats = []
-        all_squared = []
+        all_turned = []
+        all_sums = []
         for p in range(PIECES):
             in_sentence = p * PIECE % TOKENS
 
@@ -77,23 +78,30 @@ def tile_transformertranslator_kernel(tc, table, pe, bp, gamma, beta, offs, out)
                 added[:, in_sentence : in_sentence + PIECE],
                 ALU.add,
             )
-            stats = psum.tile([FEATURES, 2 * PIECE], F32, name="stats")
-            nc.tensor.matmul(stats[:, 0:PIECE], centre[:], doubled[:], start=True, stop=True)
-            squared = work.tile([FEATURES, PIECE], F32, name="squared")
-            nc.scalar.activation(squared[:], stats[:, 0:PIECE], FUNC.Square)
-            all_stats.append(stats)
-            all_squared.append(squared)
+            turned = psum.tile([PIECE, 2 * FEATURES], F32, name="turned")
+            nc.tensor.matmul(turned[:, 0:FEATURES], doubled[:], centre[:], start=True, stop=True)
+            squares = work.tile([PIECE, FEATURES], F32, name="squares")
+            sum_of_squares = work.tile([PIECE, 1], F32, name="sum_of_squares")
+            nc.scalar.activation(
+                squares[:], turned[:, 0:FEATURES], FUNC.Square, accum_out=sum_of_squares[:]
+            )
+            all_turned.append(turned)
+            all_sums.append(sum_of_squares)
 
         for p in range(PIECES):
-            centred = all_stats[p][:, 0:PIECE]
-            var = all_stats[p][:, PIECE : 2 * PIECE]
-            nc.tensor.matmul(var, average[:], all_squared[p][:], start=True, stop=True)
-            rstd = work.tile([FEATURES, PIECE], F32, name="rstd")
-            nc.scalar.activation(rstd[:], var, FUNC.Abs_reciprocal_sqrt, bias=four_eps[:, 0:1])
-            normed = work.tile([FEATURES, PIECE], F32, name="normed")
-            nc.vector.tensor_tensor(normed[:], centred, rstd[:], ALU.mult)
-            result = work.tile([FEATURES, PIECE], F32, name="result")
-            nc.vector.tensor_scalar(
-                result[:], normed[:], gain[:, 0:1], shift[:, 0:1], ALU.mult, ALU.add
+            centred_t = all_turned[p][:, 0:FEATURES]
+            normed = all_turned[p][:, FEATURES : 2 * FEATURES]
+            rstd = work.tile([PIECE, 1], F32, name="rstd")
+            nc.scalar.activation(
+                rstd[:],
+                all_sums[p][:],
+                FUNC.Abs_reciprocal_sqrt,
+                bias=four_eps[:, 0:1],
+                scale=1.0 / FEATURES,
             )
+            normed_t = work.tile([PIECE, FEATURES], F32, name="normed_t")
+            nc.vector.tensor_scalar(normed_t[:], centred_t, rstd[:, 0:1], None, ALU.mult)
+            nc.tensor.transpose(normed, normed_t[:], identity[:])
+            result = work.tile([FEATURES, PIECE], F32, name="result")
+            nc.vector.tensor_scalar(result[:], normed, gain[:, 0:1], shift[:, 0:1], ALU.mult, ALU.add)
             nc.sync.dma_start(out[:, p * PIECE : (p + 1) * PIECE], result[:])

@@ -103,5 +103,12 @@ def tile_transformertranslator_kernel(tc, table, pe, bp, gamma, beta, offs, out)
             nc.vector.tensor_scalar(normed_t[:], centred_t, rstd[:, 0:1], None, ALU.mult)
             nc.tensor.transpose(normed, normed_t[:], identity[:])
             result = work.tile([FEATURES, PIECE], F32, name="result")
-            nc.vector.tensor_scalar(result[:], normed, gain[:, 0:1], shift[:, 0:1], ALU.mult, ALU.add)
+            if p % 2 == 1:
+                nc.scalar.activation(
+                    result[:], normed, FUNC.Identity, bias=shift[:, 0:1], scale=gain[:, 0:1]
+                )
+            else:
+                nc.vector.tensor_scalar(
+                    result[:], normed, gain[:, 0:1], shift[:, 0:1], ALU.mult, ALU.add
+                )
             nc.sync.dma_start(out[:, p * PIECE : (p + 1) * PIECE], result[:])

@@ -65,28 +65,34 @@ def tile_transformertranslator_kernel(tc, table, pe, bp, gamma, beta, offs, out)
         added = held.tile([FEATURES, TOKENS], F32, name="added")
         nc.vector.tensor_scalar(added[:], position[:], bias[:, 0:1], 2.0, ALU.add, ALU.mult)
 
-        columns = PIECE // OFFSETS_PER_COLUMN
+        spans = [(s * TOKENS, TOKENS) for s in range(SENTENCES - 1)]
+        spans += [((SENTENCES - 1) * TOKENS + h * PIECE, PIECE) for h in range(TOKENS // PIECE)]
         all_turned = []
         all_sums = []
-        for p in range(PIECES):
-            in_sentence = p * PIECE % TOKENS
+        for first, count in spans:
+            in_sentence = first % TOKENS
 
-            doubled = work.tile([FEATURES, PIECE], F32, name="doubled")
+            doubled = work.tile([FEATURES, TOKENS], F32, name="doubled")
             nc.vector.tensor_tensor(
-                doubled[:],
-                words[:].indirect(offsets[:, p * columns : (p + 1) * columns]),
-                added[:, in_sentence : in_sentence + PIECE],
+                doubled[:, 0:count],
+                words[:].indirect(
+                    offsets[:, first // OFFSETS_PER_COLUMN : (first + count) // OFFSETS_PER_COLUMN]
+                ),
+                added[:, in_sentence : in_sentence + count],
                 ALU.add,
             )
-            turned = psum.tile([PIECE, 2 * FEATURES], F32, name="turned")
-            nc.tensor.matmul(turned[:, 0:FEATURES], doubled[:], centre[:], start=True, stop=True)
-            squares = work.tile([PIECE, FEATURES], F32, name="squares")
-            sum_of_squares = work.tile([PIECE, 1], F32, name="sum_of_squares")
-            nc.scalar.activation(
-                squares[:], turned[:, 0:FEATURES], FUNC.Square, accum_out=sum_of_squares[:]
-            )
-            all_turned.append(turned)
-            all_sums.append(sum_of_squares)
+            for start in range(0, count, PIECE):
+                turned = psum.tile([PIECE, 2 * FEATURES], F32, name="turned")
+                nc.tensor.matmul(
+                    turned[:, 0:FEATURES], doubled[:, start : start + PIECE], centre[:], start=True, stop=True
+                )
+                squares = work.tile([PIECE, FEATURES], F32, name="squares")
+                sum_of_squares = work.tile([PIECE, 1], F32, name="sum_of_squares")
+                nc.scalar.activation(
+                    squares[:], turned[:, 0:FEATURES], FUNC.Square, accum_out=sum_of_squares[:]
+                )
+                all_turned.append(turned)
+                all_sums.append(sum_of_squares)
 
         for p in range(PIECES):
             centred_t = all_turned[p][:, 0:FEATURES]

@@ -106,15 +106,17 @@ def tile_transformertranslator_kernel(tc, table, pe, bp, gamma, beta, offs, out)
                 scale=1.0 / FEATURES,
             )
             normed_t = work.tile([PIECE, FEATURES], F32, name="normed_t")
-            nc.vector.tensor_scalar(normed_t[:], centred_t, rstd[:, 0:1], None, ALU.mult)
-            nc.tensor.transpose(normed, normed_t[:], identity[:])
             result = work.tile([FEATURES, PIECE], F32, name="result")
-            if p % 2 == 1:
-                nc.scalar.activation(
-                    result[:], normed, FUNC.Identity, bias=shift[:, 0:1], scale=gain[:, 0:1]
-                )
-            else:
+            if p < PIECES - TOKENS // PIECE:
+                nc.vector.tensor_scalar(normed_t[:], centred_t, rstd[:, 0:1], None, ALU.mult)
+                nc.tensor.transpose(normed, normed_t[:], identity[:])
                 nc.vector.tensor_scalar(
                     result[:], normed, gain[:, 0:1], shift[:, 0:1], ALU.mult, ALU.add
+                )
+            else:
+                nc.scalar.activation(normed_t[:], centred_t, FUNC.Identity, scale=rstd[:, 0:1])
+                nc.tensor.transpose(normed, normed_t[:], identity[:])
+                nc.scalar.activation(
+                    result[:], normed, FUNC.Identity, bias=shift[:, 0:1], scale=gain[:, 0:1]
                 )
             nc.sync.dma_start(out[:, p * PIECE : (p + 1) * PIECE], result[:])

@@ -94,6 +94,7 @@ def tile_transformertranslator_kernel(tc, table, pe, bp, gamma, beta, offs, out)
                 all_turned.append(turned)
                 all_sums.append(sum_of_squares)
 
+        last_result = held.tile([FEATURES, TOKENS], F32, name="last_result")
         for p in range(PIECES):
             centred_t = all_turned[p][:, 0:FEATURES]
             normed = all_turned[p][:, FEATURES : 2 * FEATURES]
@@ -106,17 +107,23 @@ def tile_transformertranslator_kernel(tc, table, pe, bp, gamma, beta, offs, out)
                 scale=1.0 / FEATURES,
             )
             normed_t = work.tile([PIECE, FEATURES], F32, name="normed_t")
-            result = work.tile([FEATURES, PIECE], F32, name="result")
             if p < PIECES - TOKENS // PIECE:
                 nc.vector.tensor_scalar(normed_t[:], centred_t, rstd[:, 0:1], None, ALU.mult)
                 nc.tensor.transpose(normed, normed_t[:], identity[:])
+                result = work.tile([FEATURES, PIECE], F32, name="result")
                 nc.vector.tensor_scalar(
                     result[:], normed, gain[:, 0:1], shift[:, 0:1], ALU.mult, ALU.add
                 )
+                nc.sync.dma_start(out[:, p * PIECE : (p + 1) * PIECE], result[:])
             else:
                 nc.scalar.activation(normed_t[:], centred_t, FUNC.Identity, scale=rstd[:, 0:1])
                 nc.tensor.transpose(normed, normed_t[:], identity[:])
+                half = p % (TOKENS // PIECE)
                 nc.scalar.activation(
-                    result[:], normed, FUNC.Identity, bias=shift[:, 0:1], scale=gain[:, 0:1]
+                    last_result[:, half * PIECE : (half + 1) * PIECE],
+                    normed,
+                    FUNC.Identity,
+                    bias=shift[:, 0:1],
+                    scale=gain[:, 0:1],
                 )
-            nc.sync.dma_start(out[:, p * PIECE : (p + 1) * PIECE], result[:])
+        nc.sync.dma_start(out[:, (SENTENCES - 1) * TOKENS : SENTENCES * TOKENS], last_result[:])

import concourse.mybir as mybir
from concourse.masks import make_identity

F32 = mybir.dt.float32
U16 = mybir.dt.uint16
ALU = mybir.AluOpType
FUNC = mybir.ActivationFunctionType

FEATURES = 128
WORDS = 1024
TOKENS = 256
SENTENCES = 4
EPS = 1e-5
OFFSETS_PER_COLUMN = 16
PIECE = 128
PIECES = SENTENCES * TOKENS // PIECE
WARM_UP_PRODUCTS = 6

FLOPS = 2 * FEATURES * FEATURES * SENTENCES * TOKENS


def tile_transformertranslator_kernel(tc, table, pe, bp, gamma, beta, offs, out):
    nc = tc.nc
    with (
        tc.tile_pool(name="held", bufs=1) as held,
        tc.tile_pool(name="work", bufs=PIECES) as work,
        tc.psum_pool(name="psum", bufs=PIECES) as psum,
    ):
        position = held.tile([FEATURES, TOKENS], F32, name="position")
        nc.sync.dma_start(position[:], pe)
        offsets = held.tile([FEATURES, SENTENCES * TOKENS // OFFSETS_PER_COLUMN], U16, name="offsets")
        nc.sync.dma_start(offsets[:], offs)
        words = held.tile([FEATURES, WORDS], F32, name="words")
        nc.sync.dma_start(words[:], table)
        bias = held.tile([FEATURES, 1], F32, name="bias")
        nc.scalar.dma_start(bias[:], bp)
        gain = held.tile([FEATURES, 1], F32, name="gain")
        nc.scalar.dma_start(gain[:], gamma)
        shift = held.tile([FEATURES, 1], F32, name="shift")
        nc.scalar.dma_start(shift[:], beta)

        centre = held.tile([FEATURES, FEATURES], F32, name="centre")
        nc.gpsimd.memset(centre[:], -1.0 / FEATURES)
        nc.gpsimd.affine_select(
            out=centre[:],
            in_=centre[:],
            pattern=[[-1, FEATURES]],
            compare_op=ALU.not_equal,
            fill=1.0 - 1.0 / FEATURES,
            base=0,
            channel_multiplier=1,
        )
        identity = held.tile([PIECE, PIECE], F32, name="identity")
        make_identity(nc, identity[:])
        four_eps = held.tile([PIECE, 1], F32, name="four_eps")
        nc.gpsimd.memset(four_eps[:], 4.0 * EPS)

        idle_product = psum.tile([FEATURES, FEATURES], F32, name="idle_product", tag="turned")
        for repeat in range(WARM_UP_PRODUCTS):
            nc.tensor.matmul(idle_product[:], centre[:], centre[:], start=True, stop=True)

        unused = held.tile([PIECE, 1], F32, name="unused")
        nc.scalar.activation(unused[:], four_eps[:], FUNC.Abs_reciprocal_sqrt)

        added = held.tile([FEATURES, TOKENS], F32, name="added")
        nc.vector.tensor_scalar(added[:], position[:], bias[:, 0:1], 2.0, ALU.add, ALU.mult)

        spans = [(s * TOKENS, TOKENS) for s in range(SENTENCES - 1)]
        spans += [((SENTENCES - 1) * TOKENS + h * PIECE, PIECE) for h in range(TOKENS // PIECE)]
        all_turned = []
        all_sums = []
        for first, count in spans:
            in_sentence = first % TOKENS

            doubled = work.tile([FEATURES, TOKENS], F32, name="doubled")
            nc.vector.tensor_tensor(
                doubled[:, 0:count],
                words[:].indirect(
                    offsets[:, first // OFFSETS_PER_COLUMN : (first + count) // OFFSETS_PER_COLUMN]
                ),
                added[:, in_sentence : in_sentence + count],
                ALU.add,
            )
            for start in range(0, count, PIECE):
                turned = psum.tile([PIECE, 2 * FEATURES], F32, name="turned")
                nc.tensor.matmul(
                    turned[:, 0:FEATURES], doubled[:, start : start + PIECE], centre[:], start=True, stop=True
                )
                squares = work.tile([PIECE, FEATURES], F32, name="squares")
                sum_of_squares = work.tile([PIECE, 1], F32, name="sum_of_squares")
                nc.scalar.activation(
                    squares[:], turned[:, 0:FEATURES], FUNC.Square, accum_out=sum_of_squares[:]
                )
                all_turned.append(turned)
                all_sums.append(sum_of_squares)

        last_result = held.tile([FEATURES, TOKENS], F32, name="last_result")
        for p in range(PIECES):
            centred_t = all_turned[p][:, 0:FEATURES]
            normed = all_turned[p][:, FEATURES : 2 * FEATURES]
            rstd = work.tile([PIECE, 1], F32, name="rstd")
            nc.scalar.activation(
                rstd[:],
                all_sums[p][:],
                FUNC.Abs_reciprocal_sqrt,
                bias=four_eps[:, 0:1],
                scale=1.0 / FEATURES,
            )
            normed_t = work.tile([PIECE, FEATURES], F32, name="normed_t")
            if p < PIECES - TOKENS // PIECE:
                nc.vector.tensor_scalar(normed_t[:], centred_t, rstd[:, 0:1], None, ALU.mult)
                nc.tensor.transpose(normed, normed_t[:], identity[:])
                result = work.tile([FEATURES, PIECE], F32, name="result")
                nc.vector.tensor_scalar(
                    result[:], normed, gain[:, 0:1], shift[:, 0:1], ALU.mult, ALU.add
                )
                nc.sync.dma_start(out[:, p * PIECE : (p + 1) * PIECE], result[:])
            else:
                nc.scalar.activation(normed_t[:], centred_t, FUNC.Identity, scale=rstd[:, 0:1])
                nc.tensor.transpose(normed, normed_t[:], identity[:])
                half = p % (TOKENS // PIECE)
                nc.scalar.activation(
                    last_result[:, half * PIECE : (half + 1) * PIECE],
                    normed,
                    FUNC.Identity,
                    bias=shift[:, 0:1],
                    scale=gain[:, 0:1],
                )
        nc.sync.dma_start(out[:, (SENTENCES - 1) * TOKENS : SENTENCES * TOKENS], last_result[:])
